import numpy as np
import ml_dtypes


def mxq(x, axis, fmt="e4m3"):
    dtype, down = {"e4m3": (ml_dtypes.float8_e4m3fn, 7), "e5m2": (ml_dtypes.float8_e5m2, 14)}[fmt]
    v = np.moveaxis(np.asarray(x, np.float32).astype(ml_dtypes.bfloat16).astype(np.float64), axis, -1)
    blocks = v.reshape(v.shape[:-1] + (-1, 32))
    amax = np.abs(blocks).max(-1, keepdims=True)
    byte = np.maximum(np.where(amax > 0, np.frexp(amax)[1] - 1 + 127, 0) - down, 1)
    scale = np.exp2(byte - 127.0)
    codes = (blocks / scale).astype(np.float32).astype(dtype).astype(np.float64)
    return np.moveaxis((codes * scale).reshape(v.shape), -1, axis)


WIDE = False


def mx_kscale(k):
    if not WIDE:
        return np.ones(k)
    levels = np.array([10, -10, 5, -5, 0])
    if k % 512:
        return np.exp2(np.random.permutation(np.resize(levels, k // 32))).repeat(32)
    a = np.empty((k // 512, 16))
    for p in range(k // 512):
        a[p, :8] = np.random.permutation(np.resize(levels, 8))
        for g in range(8):
            far = levels[np.abs(levels - a[p, g]) >= 10]
            a[p, g + 8] = far[np.random.randint(len(far))]
    return np.exp2(a.ravel()).repeat(32)


BF16 = ml_dtypes.bfloat16


def bf(x):
    return np.asarray(x, np.float32).astype(BF16)


def f64(x):
    return np.asarray(x).astype(np.float64)


B, IN, H, Z, G = 512, 512, 1024, 256, 4


def gate_scales(zx, dx_w):
    return (f64(zx).transpose(1, 0, 2) @ f64(dx_w).transpose(0, 2, 1)).transpose(1, 0, 2)


def setup_inputs():
    s = mx_kscale(B)
    u = mx_kscale(G * H).reshape(G, H)
    src_x0 = bf(np.random.standard_normal((B, IN)))
    zx = bf(np.random.standard_normal((B, G, Z)))
    dx_w = bf(np.random.standard_normal((G, H, Z)) / np.sqrt(Z))
    w_x0 = bf(np.random.standard_normal((G, H, IN)) / np.sqrt(IN))
    g = bf(np.random.standard_normal((B, G, H)) * np.exp2(np.random.randint(-6, 1, (B, 1, 1))) * 4.0
           / s[:, None, None] * u[None, :, :])
    d_x = gate_scales(zx, dx_w)
    return {"src_x": bf(f64(src_x0) * s[:, None]), "zx": zx, "dx_w": dx_w,
            "w_x": bf(f64(w_x0) / u[:, :, None]),
            "d_x": np.asarray(d_x, np.float32), "grad_out": g}


def reference(src_x, zx, dx_w, w_x, d_x, grad_out):
    dwx = (f64(grad_out) * f64(d_x)).reshape(B, G * H)
    dsrc = mxq(dwx, 1, "e5m2") @ mxq(f64(w_x).reshape(G * H, IN), 0, "e4m3")
    dw = mxq(dwx, 0, "e5m2").T @ mxq(f64(src_x), 0, "e4m3")
    return dsrc, dw.reshape(G, H, IN)

@@ -1,0 +1,172 @@
+from contextlib import ExitStack
+
+import concourse.mybir as mybir
+from concourse.masks import make_identity
+
+B, IN, GH = 512, 512, 4096
+
+FLOPS = 2 * 2 * B * GH * IN
+BYTES = B * GH * 2 + B * GH * 4 + GH * IN * 2 + B * IN * 2 + B * IN * 4 + GH * IN * 4
+
+F32 = mybir.dt.float32
+BF16 = mybir.dt.bfloat16
+U32 = mybir.dt.uint32
+U8 = mybir.dt.uint8
+E4X4 = mybir.dt.float8_e4m3fn_x4
+E5X4 = mybir.dt.float8_e5m2_x4
+
+P = 128
+PACK = 4
+CH = 512
+NCH = GH // CH
+LOAD_GROUPS = (1, 1, 1, 1, 2, 2)
+V_EVAC = ()
+
+
+def tile_metalstmcell_pa_v_kernel(tc, src_x, zx, dx_w, w_x, d_x, grad_out, out_0, out_1):
+    nc = tc.nc
+
+    g_hbm = grad_out.rearrange("b g h -> b (g h)").rearrange("(p j) w -> p j w", j=PACK)
+    d_hbm = d_x.rearrange("b g h -> b (g h)").rearrange("(p j) w -> p j w", j=PACK)
+    w_hbm = w_x.rearrange("g h i -> (g h) i").rearrange("(c p j) i -> p c j i", p=P, j=PACK)
+    s_hbm = src_x.rearrange("(p j) i -> p j i", j=PACK)
+    o0_hbm = out_0.rearrange("(p j) i -> p j i", j=PACK)
+    o1_hbm = out_1.rearrange("g h i -> (g h) i").rearrange("(c a m) i -> m c a i", a=PACK, m=P)
+
+    with ExitStack() as ctx:
+        const = ctx.enter_context(tc.tile_pool(name="const", bufs=1))
+        inp = ctx.enter_context(tc.tile_pool(name="inp", bufs=1))
+        slot = ctx.enter_context(tc.tile_pool(name="slot", bufs=8))
+        work3 = ctx.enter_context(tc.tile_pool(name="work3", bufs=3))
+        work2 = ctx.enter_context(tc.tile_pool(name="work2", bufs=2))
+        ps_acc = ctx.enter_context(tc.psum_pool(name="ps_acc", bufs=1))
+        ps_t = ctx.enter_context(tc.psum_pool(name="ps_t", bufs=2))
+        ps_o = ctx.enter_context(tc.psum_pool(name="ps_o", bufs=2))
+
+        ident = const.tile([P, P], F32, name="ident")
+        make_identity(nc, ident[:])
+
+        g_of, d_of, w_of = [], [], []
+        src_raw = inp.tile([P, PACK, IN], BF16, name="src_raw")
+        c = 0
+        for n in LOAD_GROUPS:
+            cols = slice(c * CH, (c + n) * CH)
+            g_t = inp.tile([P, PACK, n * CH], BF16, name="g%d" % c)
+            nc.sync.dma_start(out=g_t[:], in_=g_hbm[:, :, cols])
+            if n == 1:
+                d_t = slot.tile([P, PACK, CH], F32, name="d%d" % c, tag="slot")
+            else:
+                d_t = inp.tile([P, PACK, n * CH], F32, name="d%d" % c)
+            nc.sync.dma_start(out=d_t[:], in_=d_hbm[:, :, cols])
+            if c == 0:
+                nc.sync.dma_start(out=src_raw[:], in_=s_hbm)
+            w_t = inp.tile([P, n, PACK, IN], BF16, name="w%d" % c)
+            nc.sync.dma_start(out=w_t[:], in_=w_hbm[:, c : c + n])
+            for k in range(n):
+                g_of.append(g_t[:, :, k * CH : (k + 1) * CH])
+                d_of.append(d_t[:, :, k * CH : (k + 1) * CH])
+                w_of.append(w_t[:, k])
+            c += n
+
+        acc = [ps_acc.tile([P, IN], F32, name="acc%d" % j) for j in range(PACK)]
+        src_codes = const.tile([P, IN], U32, name="src_codes", align_bytes=64)
+        src_scales = const.tile([P, IN], U8, name="src_scales", align_bytes=64)
+
+        dz, xts, dzt, dzi, wg = {}, {}, {}, {}, {}
+        tok_q, feat_q, w_q = {}, {}, {}
+
+        def mult(i):
+            dz[i] = work3.tile([P, PACK, CH], BF16, name="dz", tag="dz")
+            nc.vector.tensor_tensor(out=dz[i][:], in0=g_of[i], in1=d_of[i], op=mybir.AluOpType.mult)
+
+        def interleave_rows(eng_copy, raw):
+            grouped = work3.tile([P, IN, PACK], BF16, name="wg", tag="wg", align_bytes=64)
+            eng_copy(out=grouped[:], in_=raw.rearrange("p j w -> p w j"))
+            return grouped
+
+        def transposes(i):
+            xts[i] = []
+            for h in range(2):
+                xt = ps_t.tile([P, 2, 2, P], F32, name="xt", tag="xt")
+                for jj in range(2):
+                    words = dz[i][:, 2 * h + jj, :].bitcast(F32)
+                    for u in range(2):
+                        nc.tensor.transpose(xt[:, jj, u, :], words[:, u : CH // 2 : 2], ident[:])
+                xts[i].append(xt)
+
+        def copy_transposed(i):
+            dzt[i] = work2.tile([P, B, PACK], BF16, name="dzt", tag="dzt", align_bytes=64)
+            tw = dzt[i][:].rearrange("p c t -> p (c t)").bitcast(F32).rearrange("p (j r u) -> p j r u", j=PACK, u=2)
+            for h in range(2):
+                nc.scalar.copy(out=tw[:, 2 * h : 2 * h + 2], in_=xts[i][h][:].rearrange("p j u r -> p j r u"))
+
+        def interleave_tokens(i):
+            dzi[i] = work2.tile([P, CH, PACK], BF16, name="dzi", tag="dzi", align_bytes=64)
+            nc.vector.tensor_copy(out=dzi[i][:], in_=dz[i][:].rearrange("p j w -> p w j"))
+
+        def quantize(grouped, fmt, kind):
+            codes = work2.tile([P, CH], U32, name="c" + kind, tag="c" + kind, align_bytes=64)
+            scales = work2.tile([P, CH], U8, name="s" + kind, tag="s" + kind, align_bytes=64)
+            nc.vector.quantize_mx(out=codes[:].bitcast(fmt), scales=scales[:], in_=grouped[:].rearrange("p w j -> p (w j)"))
+            return codes, scales
+
+        def out0_pass(i):
+            codes, scales = feat_q[i]
+            wc, ws = w_q[i]
+            for j in range(PACK):
+                m = slice(j * P, (j + 1) * P)
+                nc.tensor.matmul_mx(
+                    out=acc[j][:],
+                    lhsT=codes[:, m].bitcast(E5X4),
+                    lhsT_scale=scales[:, m],
+                    rhs=wc[:].bitcast(E4X4),
+                    rhs_scale=ws[:],
+                    start=(i == 0),
+                    stop=(i == NCH - 1),
+                )
+
+        def out1_tiles(i):
+            codes, scales = tok_q[i]
+            stage = slot.tile([P, PACK, IN], F32, name="stage", tag="slot")
+            for a in range(PACK):
+                m = slice(a * P, (a + 1) * P)
+                o1 = ps_o.tile([P, IN], F32, name="o1", tag="o1")
+                nc.tensor.matmul_mx(
+                    out=o1[:],
+                    lhsT=codes[:, m].bitcast(E5X4),
+                    lhsT_scale=scales[:, m],
+                    rhs=src_codes[:].bitcast(E4X4),
+                    rhs_scale=src_scales[:],
+                    start=True,
+                    stop=True,
+                )
+                nc.scalar.copy(out=stage[:, a, :], in_=o1[:])
+            nc.sync.dma_start(out=o1_hbm[:, i], in_=stage[:])
+
+        with tc.manual_schedule():
+            src_g = interleave_rows(nc.scalar.copy, src_raw[:])
+            for i in range(NCH + 1):
+                if i < NCH:
+                    mult(i)
+                    wg[i] = interleave_rows(nc.scalar.copy, w_of[i])
+                    transposes(i)
+                    copy_transposed(i)
+                if i >= 1:
+                    feat_q[i - 1] = quantize(dzt[i - 1], E5X4, "f")
+                if i < NCH:
+                    interleave_tokens(i)
+                if i == 0:
+                    nc.vector.quantize_mx(
+                        out=src_codes[:].bitcast(E4X4), scales=src_scales[:], in_=src_g[:].rearrange("p w j -> p (w j)")
+                    )
+                else:
+                    w_q[i - 1] = quantize(wg[i - 1], E4X4, "w")
+                    out0_pass(i - 1)
+                if i < NCH:
+                    tok_q[i] = quantize(dzi[i], E5X4, "t")
+                    out1_tiles(i)
+
+            stage0 = slot.tile([P, PACK, IN], F32, name="stage0", tag="slot")
+            for j in range(PACK):
+                nc.vector.tensor_copy(out=stage0[:, j, :], in_=acc[j][:])
+            nc.sync.dma_start(out=o0_hbm, in_=stage0[:])

@@ -31,7 +31,7 @@ def tile_metalstmcell_pa_v_kernel(tc, src_x, zx, dx_w, w_x, d_x, grad_out, out_0
     w_hbm = w_x.rearrange("g h i -> (g h) i").rearrange("(c p j) i -> p c j i", p=P, j=PACK)
     s_hbm = src_x.rearrange("(p j) i -> p j i", j=PACK)
     o0_hbm = out_0.rearrange("(p j) i -> p j i", j=PACK)
-    o1_hbm = out_1.rearrange("g h i -> (g h) i").rearrange("(c a m) i -> m c a i", a=PACK, m=P)
+    o1_hbm = out_1.rearrange("g h i -> (g h) i").rearrange("(c m a) i -> m c a i", a=PACK, m=P)
 
     with ExitStack() as ctx:
         const = ctx.enter_context(tc.tile_pool(name="const", bufs=1))
@@ -49,22 +49,32 @@ def tile_metalstmcell_pa_v_kernel(tc, src_x, zx, dx_w, w_x, d_x, grad_out, out_0
         g_of, d_of, w_of = [], [], []
         src_raw = inp.tile([P, PACK, IN], BF16, name="src_raw")
         c = 0
+        g0_rows, d0_rows = [], []
         for n in LOAD_GROUPS:
             cols = slice(c * CH, (c + n) * CH)
-            g_t = inp.tile([P, PACK, n * CH], BF16, name="g%d" % c)
-            nc.sync.dma_start(out=g_t[:], in_=g_hbm[:, :, cols])
-            if n == 1:
-                d_t = slot.tile([P, PACK, CH], F32, name="d%d" % c, tag="slot")
-            else:
-                d_t = inp.tile([P, PACK, n * CH], F32, name="d%d" % c)
-            nc.sync.dma_start(out=d_t[:], in_=d_hbm[:, :, cols])
             if c == 0:
+                for j in range(PACK):
+                    g_r = inp.tile([P, CH], BF16, name="g0r%d" % j)
+                    nc.sync.dma_start(out=g_r[:], in_=g_hbm[:, j, cols])
+                    d_r = inp.tile([P, CH], F32, name="d0r%d" % j)
+                    nc.sync.dma_start(out=d_r[:], in_=d_hbm[:, j, cols])
+                    g0_rows.append(g_r)
+                    d0_rows.append(d_r)
+                g_t, d_t = None, None
                 nc.sync.dma_start(out=src_raw[:], in_=s_hbm)
+            else:
+                g_t = inp.tile([P, PACK, n * CH], BF16, name="g%d" % c)
+                nc.sync.dma_start(out=g_t[:], in_=g_hbm[:, :, cols])
+                if n == 1:
+                    d_t = slot.tile([P, PACK, CH], F32, name="d%d" % c, tag="slot")
+                else:
+                    d_t = inp.tile([P, PACK, n * CH], F32, name="d%d" % c)
+                nc.sync.dma_start(out=d_t[:], in_=d_hbm[:, :, cols])
             w_t = inp.tile([P, n, PACK, IN], BF16, name="w%d" % c)
             nc.sync.dma_start(out=w_t[:], in_=w_hbm[:, c : c + n])
             for k in range(n):
-                g_of.append(g_t[:, :, k * CH : (k + 1) * CH])
-                d_of.append(d_t[:, :, k * CH : (k + 1) * CH])
+                g_of.append(None if c == 0 else g_t[:, :, k * CH : (k + 1) * CH])
+                d_of.append(None if c == 0 else d_t[:, :, k * CH : (k + 1) * CH])
                 w_of.append(w_t[:, k])
             c += n
 
@@ -77,11 +87,18 @@ def tile_metalstmcell_pa_v_kernel(tc, src_x, zx, dx_w, w_x, d_x, grad_out, out_0
 
         def mult(i):
             dz[i] = work3.tile([P, PACK, CH], BF16, name="dz", tag="dz")
-            nc.vector.tensor_tensor(out=dz[i][:], in0=g_of[i], in1=d_of[i], op=mybir.AluOpType.mult)
+            if i == 0:
+                for j in range(PACK):
+                    nc.vector.tensor_tensor(out=dz[i][:, j, :], in0=g0_rows[j][:], in1=d0_rows[j][:], op=mybir.AluOpType.mult)
+            else:
+                nc.vector.tensor_tensor(out=dz[i][:], in0=g_of[i], in1=d_of[i], op=mybir.AluOpType.mult)
 
         def interleave_rows(eng_copy, raw):
             grouped = work3.tile([P, IN, PACK], BF16, name="wg", tag="wg", align_bytes=64)
-            eng_copy(out=grouped[:], in_=raw.rearrange("p j w -> p w j"))
+            eng_copy(
+                out=grouped[:].rearrange("p (c i) t -> p c t i", i=4),
+                in_=raw.rearrange("p t (c i) -> p c t i", i=4),
+            )
             return grouped
 
         def transposes(i):
@@ -102,7 +119,10 @@ def tile_metalstmcell_pa_v_kernel(tc, src_x, zx, dx_w, w_x, d_x, grad_out, out_0
 
         def interleave_tokens(i):
             dzi[i] = work2.tile([P, CH, PACK], BF16, name="dzi", tag="dzi", align_bytes=64)
-            nc.vector.tensor_copy(out=dzi[i][:], in_=dz[i][:].rearrange("p j w -> p w j"))
+            nc.vector.tensor_copy(
+                out=dzi[i][:].rearrange("p (a m) j -> p m j a", a=PACK),
+                in_=dz[i][:].rearrange("p j (m a) -> p m j a", a=PACK),
+            )
 
         def quantize(grouped, fmt, kind):
             codes = work2.tile([P, CH], U32, name="c" + kind, tag="c" + kind, align_bytes=64)
@@ -125,48 +145,71 @@ def tile_metalstmcell_pa_v_kernel(tc, src_x, zx, dx_w, w_x, d_x, grad_out, out_0
                     stop=(i == NCH - 1),
                 )
 
-        def out1_tiles(i):
-            codes, scales = tok_q[i]
-            stage = slot.tile([P, PACK, IN], F32, name="stage", tag="slot")
-            for a in range(PACK):
-                m = slice(a * P, (a + 1) * P)
-                o1 = ps_o.tile([P, IN], F32, name="o1", tag="o1")
-                nc.tensor.matmul_mx(
-                    out=o1[:],
-                    lhsT=codes[:, m].bitcast(E5X4),
-                    lhsT_scale=scales[:, m],
-                    rhs=src_codes[:].bitcast(E4X4),
-                    rhs_scale=src_scales[:],
-                    start=True,
-                    stop=True,
-                )
-                nc.scalar.copy(out=stage[:, a, :], in_=o1[:])
-            nc.sync.dma_start(out=o1_hbm[:, i], in_=stage[:])
+        stages = {}
 
+        def out1_tile(i, a, eng_copy):
+            codes, scales = tok_q[i]
+            if a == 0:
+                stages[i] = slot.tile([P, PACK, IN], F32, name="stage", tag="slot")
+            m = slice(a * P, (a + 1) * P)
+            o1 = ps_o.tile([P, IN], F32, name="o1", tag="o1")
+            nc.tensor.matmul_mx(
+                out=o1[:],
+                lhsT=codes[:, m].bitcast(E5X4),
+                lhsT_scale=scales[:, m],
+                rhs=src_codes[:].bitcast(E4X4),
+                rhs_scale=src_scales[:],
+                start=True,
+                stop=True,
+            )
+            return o1
+
+        def evac1(i, a, o1, eng_copy):
+            eng_copy(out=stages[i][:, a, :], in_=o1[:])
+
+        LAST = NCH - 1
         with tc.manual_schedule():
-            src_g = interleave_rows(nc.scalar.copy, src_raw[:])
-            for i in range(NCH + 1):
-                if i < NCH:
-                    mult(i)
+            for i in range(NCH):
+                mult(i)
+                if i < LAST:
                     wg[i] = interleave_rows(nc.scalar.copy, w_of[i])
-                    transposes(i)
-                    copy_transposed(i)
+                transposes(i)
+                copy_transposed(i)
                 if i >= 1:
                     feat_q[i - 1] = quantize(dzt[i - 1], E5X4, "f")
-                if i < NCH:
-                    interleave_tokens(i)
+                interleave_tokens(i)
+                if i == 0:
+                    src_g = interleave_rows(nc.vector.tensor_copy, src_raw[:])
+                else:
+                    w_q[i - 1] = quantize(wg[i - 1], E4X4, "w")
+                    out0_pass(i - 1)
+                tok_q[i] = quantize(dzi[i], E5X4, "t")
                 if i == 0:
                     nc.vector.quantize_mx(
                         out=src_codes[:].bitcast(E4X4), scales=src_scales[:], in_=src_g[:].rearrange("p w j -> p (w j)")
                     )
-                else:
-                    w_q[i - 1] = quantize(wg[i - 1], E4X4, "w")
-                    out0_pass(i - 1)
-                if i < NCH:
-                    tok_q[i] = quantize(dzi[i], E5X4, "t")
-                    out1_tiles(i)
+                if i == LAST:
+                    wg[i] = interleave_rows(nc.vector.tensor_copy, w_of[i])
+                if i < LAST:
+                    for a in range(PACK):
+                        evac1(i, a, out1_tile(i, a, None), nc.scalar.copy)
+                    nc.sync.dma_start(out=o1_hbm[:, i], in_=stages[i][:])
 
+            for a in range(2):
+                evac1(LAST, a, out1_tile(LAST, a, None), nc.scalar.copy)
+            nc.sync.dma_start(out=o1_hbm[:, LAST, 0:2], in_=stages[LAST][:, 0:2])
+            feat_q[LAST] = quantize(dzt[LAST], E5X4, "f")
+            w_q[LAST] = quantize(wg[LAST], E4X4, "w")
+            out0_pass(LAST)
+            o1_2 = out1_tile(LAST, 2, None)
+            o1_3 = out1_tile(LAST, 3, None)
             stage0 = slot.tile([P, PACK, IN], F32, name="stage0", tag="slot")
-            for j in range(PACK):
-                nc.vector.tensor_copy(out=stage0[:, j, :], in_=acc[j][:])
-            nc.sync.dma_start(out=o0_hbm, in_=stage0[:])
+            nc.vector.tensor_copy(out=stage0[:, 0, :], in_=acc[0][:])
+            nc.scalar.copy(out=stage0[:, 2, :], in_=acc[2][:])
+            nc.vector.tensor_copy(out=stage0[:, 1, :], in_=acc[1][:])
+            nc.scalar.copy(out=stage0[:, 3, :], in_=acc[3][:])
+            nc.sync.dma_start(out=o0_hbm[:, 0:2], in_=stage0[:, 0:2])
+            nc.sync.dma_start(out=o0_hbm[:, 2:4], in_=stage0[:, 2:4])
+            evac1(LAST, 2, o1_2, nc.vector.tensor_copy)
+            evac1(LAST, 3, o1_3, nc.scalar.copy)
+            nc.sync.dma_start(out=o1_hbm[:, LAST, 2:4], in_=stages[LAST][:, 2:4])

@@ -19,7 +19,7 @@ P = 128
 PACK = 4
 CH = 512
 NCH = GH // CH
-LOAD_GROUPS = (1, 1, 1, 1, 2, 2)
+LOAD_GROUPS = (1, 1, 1, 1, 1, 1, 1, 1)
 V_EVAC = ()
 
 
@@ -36,7 +36,7 @@ def tile_metalstmcell_pa_v_kernel(tc, src_x, zx, dx_w, w_x, d_x, grad_out, out_0
     with ExitStack() as ctx:
         const = ctx.enter_context(tc.tile_pool(name="const", bufs=1))
         inp = ctx.enter_context(tc.tile_pool(name="inp", bufs=1))
-        slot = ctx.enter_context(tc.tile_pool(name="slot", bufs=8))
+        slot = ctx.enter_context(tc.tile_pool(name="slot", bufs=10))
         work3 = ctx.enter_context(tc.tile_pool(name="work3", bufs=3))
         work2 = ctx.enter_context(tc.tile_pool(name="work2", bufs=2))
         ps_acc = ctx.enter_context(tc.psum_pool(name="ps_acc", bufs=1))

@@ -19,7 +19,7 @@ P = 128
 PACK = 4
 CH = 512
 NCH = GH // CH
-LOAD_GROUPS = (1, 1, 1, 1, 1, 1, 1, 1)
+LOAD_GROUPS = (2, 2, 2, 2)
 V_EVAC = ()
 
 
@@ -36,8 +36,8 @@ def tile_metalstmcell_pa_v_kernel(tc, src_x, zx, dx_w, w_x, d_x, grad_out, out_0
     with ExitStack() as ctx:
         const = ctx.enter_context(tc.tile_pool(name="const", bufs=1))
         inp = ctx.enter_context(tc.tile_pool(name="inp", bufs=1))
-        slot = ctx.enter_context(tc.tile_pool(name="slot", bufs=10))
-        work3 = ctx.enter_context(tc.tile_pool(name="work3", bufs=3))
+        slot = ctx.enter_context(tc.tile_pool(name="slot", bufs=6))
+        work3 = ctx.enter_context(tc.tile_pool(name="work3", bufs=2))
         work2 = ctx.enter_context(tc.tile_pool(name="work2", bufs=2))
         ps_acc = ctx.enter_context(tc.psum_pool(name="ps_acc", bufs=1))
         ps_t = ctx.enter_context(tc.psum_pool(name="ps_t", bufs=2))
@@ -54,9 +54,9 @@ def tile_metalstmcell_pa_v_kernel(tc, src_x, zx, dx_w, w_x, d_x, grad_out, out_0
             cols = slice(c * CH, (c + n) * CH)
             if c == 0:
                 for j in range(PACK):
-                    g_r = inp.tile([P, CH], BF16, name="g0r%d" % j)
+                    g_r = inp.tile([P, n * CH], BF16, name="g0r%d" % j)
                     nc.sync.dma_start(out=g_r[:], in_=g_hbm[:, j, cols])
-                    d_r = inp.tile([P, CH], F32, name="d0r%d" % j)
+                    d_r = inp.tile([P, n * CH], F32, name="d0r%d" % j)
                     nc.sync.dma_start(out=d_r[:], in_=d_hbm[:, j, cols])
                     g0_rows.append(g_r)
                     d0_rows.append(d_r)
@@ -87,9 +87,12 @@ def tile_metalstmcell_pa_v_kernel(tc, src_x, zx, dx_w, w_x, d_x, grad_out, out_0
 
         def mult(i):
             dz[i] = work3.tile([P, PACK, CH], BF16, name="dz", tag="dz")
-            if i == 0:
+            if g_of[i] is None:
+                lo = i * CH
                 for j in range(PACK):
-                    nc.vector.tensor_tensor(out=dz[i][:, j, :], in0=g0_rows[j][:], in1=d0_rows[j][:], op=mybir.AluOpType.mult)
+                    nc.vector.tensor_tensor(
+                        out=dz[i][:, j, :], in0=g0_rows[j][:, lo : lo + CH], in1=d0_rows[j][:, lo : lo + CH], op=mybir.AluOpType.mult
+                    )
             else:
                 nc.vector.tensor_tensor(out=dz[i][:], in0=g_of[i], in1=d_of[i], op=mybir.AluOpType.mult)
 
@@ -197,7 +200,6 @@ def tile_metalstmcell_pa_v_kernel(tc, src_x, zx, dx_w, w_x, d_x, grad_out, out_0
 
             for a in range(2):
                 evac1(LAST, a, out1_tile(LAST, a, None), nc.scalar.copy)
-            nc.sync.dma_start(out=o1_hbm[:, LAST, 0:2], in_=stages[LAST][:, 0:2])
             feat_q[LAST] = quantize(dzt[LAST], E5X4, "f")
             w_q[LAST] = quantize(wg[LAST], E4X4, "w")
             out0_pass(LAST)
@@ -208,8 +210,7 @@ def tile_metalstmcell_pa_v_kernel(tc, src_x, zx, dx_w, w_x, d_x, grad_out, out_0
             nc.scalar.copy(out=stage0[:, 2, :], in_=acc[2][:])
             nc.vector.tensor_copy(out=stage0[:, 1, :], in_=acc[1][:])
             nc.scalar.copy(out=stage0[:, 3, :], in_=acc[3][:])
-            nc.sync.dma_start(out=o0_hbm[:, 0:2], in_=stage0[:, 0:2])
-            nc.sync.dma_start(out=o0_hbm[:, 2:4], in_=stage0[:, 2:4])
+            nc.sync.dma_start(out=o0_hbm, in_=stage0[:])
             evac1(LAST, 2, o1_2, nc.vector.tensor_copy)
             evac1(LAST, 3, o1_3, nc.scalar.copy)
-            nc.sync.dma_start(out=o1_hbm[:, LAST, 2:4], in_=stages[LAST][:, 2:4])
+            nc.sync.dma_start(out=o1_hbm[:, LAST], in_=stages[LAST][:])

@@ -19,7 +19,7 @@ P = 128
 PACK = 4
 CH = 512
 NCH = GH // CH
-LOAD_GROUPS = (2, 2, 2, 2)
+LOAD_GROUPS = (1, 1, 1, 1, 2, 2)
 V_EVAC = ()
 
 
@@ -36,8 +36,8 @@ def tile_metalstmcell_pa_v_kernel(tc, src_x, zx, dx_w, w_x, d_x, grad_out, out_0
     with ExitStack() as ctx:
         const = ctx.enter_context(tc.tile_pool(name="const", bufs=1))
         inp = ctx.enter_context(tc.tile_pool(name="inp", bufs=1))
-        slot = ctx.enter_context(tc.tile_pool(name="slot", bufs=6))
-        work3 = ctx.enter_context(tc.tile_pool(name="work3", bufs=2))
+        slot = ctx.enter_context(tc.tile_pool(name="slot", bufs=8))
+        work3 = ctx.enter_context(tc.tile_pool(name="work3", bufs=3))
         work2 = ctx.enter_context(tc.tile_pool(name="work2", bufs=2))
         ps_acc = ctx.enter_context(tc.psum_pool(name="ps_acc", bufs=1))
         ps_t = ctx.enter_context(tc.psum_pool(name="ps_t", bufs=2))
@@ -54,17 +54,28 @@ def tile_metalstmcell_pa_v_kernel(tc, src_x, zx, dx_w, w_x, d_x, grad_out, out_0
             cols = slice(c * CH, (c + n) * CH)
             if c == 0:
                 for j in range(PACK):
-                    g_r = inp.tile([P, n * CH], BF16, name="g0r%d" % j)
+                    g_r = inp.tile([P, CH], BF16, name="g0r%d" % j)
                     nc.sync.dma_start(out=g_r[:], in_=g_hbm[:, j, cols])
-                    d_r = inp.tile([P, n * CH], F32, name="d0r%d" % j)
+                    d_r = inp.tile([P, CH], F32, name="d0r%d" % j)
                     nc.sync.dma_start(out=d_r[:], in_=d_hbm[:, j, cols])
                     g0_rows.append(g_r)
                     d0_rows.append(d_r)
                 g_t, d_t = None, None
                 nc.sync.dma_start(out=src_raw[:], in_=s_hbm)
             else:
-                g_t = inp.tile([P, PACK, n * CH], BF16, name="g%d" % c)
-                nc.sync.dma_start(out=g_t[:], in_=g_hbm[:, :, cols])
+                if c == 2:
+                    g_wide = inp.tile([P, PACK, 2 * CH], BF16, name="g23")
+                    nc.sync.dma_start(out=g_wide[:], in_=g_hbm[:, :, 2 * CH : 4 * CH])
+                if c == 4:
+                    g_wide4 = inp.tile([P, PACK, 4 * CH], BF16, name="g4567")
+                    nc.sync.dma_start(out=g_wide4[:], in_=g_hbm[:, :, 4 * CH : 8 * CH])
+                if c in (2, 3):
+                    g_t = g_wide[:, :, (c - 2) * CH : (c - 1) * CH]
+                elif c >= 4:
+                    g_t = g_wide4[:, :, (c - 4) * CH : (c - 4 + n) * CH]
+                else:
+                    g_t = inp.tile([P, PACK, n * CH], BF16, name="g%d" % c)
+                    nc.sync.dma_start(out=g_t[:], in_=g_hbm[:, :, cols])
                 if n == 1:
                     d_t = slot.tile([P, PACK, CH], F32, name="d%d" % c, tag="slot")
                 else:
@@ -87,12 +98,9 @@ def tile_metalstmcell_pa_v_kernel(tc, src_x, zx, dx_w, w_x, d_x, grad_out, out_0
 
         def mult(i):
             dz[i] = work3.tile([P, PACK, CH], BF16, name="dz", tag="dz")
-            if g_of[i] is None:
-                lo = i * CH
+            if i == 0:
                 for j in range(PACK):
-                    nc.vector.tensor_tensor(
-                        out=dz[i][:, j, :], in0=g0_rows[j][:, lo : lo + CH], in1=d0_rows[j][:, lo : lo + CH], op=mybir.AluOpType.mult
-                    )
+                    nc.vector.tensor_tensor(out=dz[i][:, j, :], in0=g0_rows[j][:], in1=d0_rows[j][:], op=mybir.AluOpType.mult)
             else:
                 nc.vector.tensor_tensor(out=dz[i][:], in0=g_of[i], in1=d_of[i], op=mybir.AluOpType.mult)
 
@@ -200,6 +208,7 @@ def tile_metalstmcell_pa_v_kernel(tc, src_x, zx, dx_w, w_x, d_x, grad_out, out_0
 
             for a in range(2):
                 evac1(LAST, a, out1_tile(LAST, a, None), nc.scalar.copy)
+            nc.sync.dma_start(out=o1_hbm[:, LAST, 0:2], in_=stages[LAST][:, 0:2])
             feat_q[LAST] = quantize(dzt[LAST], E5X4, "f")
             w_q[LAST] = quantize(wg[LAST], E4X4, "w")
             out0_pass(LAST)
@@ -210,7 +219,8 @@ def tile_metalstmcell_pa_v_kernel(tc, src_x, zx, dx_w, w_x, d_x, grad_out, out_0
             nc.scalar.copy(out=stage0[:, 2, :], in_=acc[2][:])
             nc.vector.tensor_copy(out=stage0[:, 1, :], in_=acc[1][:])
             nc.scalar.copy(out=stage0[:, 3, :], in_=acc[3][:])
-            nc.sync.dma_start(out=o0_hbm, in_=stage0[:])
+            nc.sync.dma_start(out=o0_hbm[:, 0:2], in_=stage0[:, 0:2])
+            nc.sync.dma_start(out=o0_hbm[:, 2:4], in_=stage0[:, 2:4])
             evac1(LAST, 2, o1_2, nc.vector.tensor_copy)
             evac1(LAST, 3, o1_3, nc.scalar.copy)
-            nc.sync.dma_start(out=o1_hbm[:, LAST], in_=stages[LAST][:])
+            nc.sync.dma_start(out=o1_hbm[:, LAST, 2:4], in_=stages[LAST][:, 2:4])

from contextlib import ExitStack

import concourse.mybir as mybir
from concourse.masks import make_identity

B, IN, GH = 512, 512, 4096

FLOPS = 2 * 2 * B * GH * IN
BYTES = B * GH * 2 + B * GH * 4 + GH * IN * 2 + B * IN * 2 + B * IN * 4 + GH * IN * 4

F32 = mybir.dt.float32
BF16 = mybir.dt.bfloat16
U32 = mybir.dt.uint32
U8 = mybir.dt.uint8
E4X4 = mybir.dt.float8_e4m3fn_x4
E5X4 = mybir.dt.float8_e5m2_x4

P = 128
PACK = 4
CH = 512
NCH = GH // CH
LOAD_GROUPS = (1, 1, 1, 1, 2, 2)
V_EVAC = ()


def tile_metalstmcell_pa_v_kernel(tc, src_x, zx, dx_w, w_x, d_x, grad_out, out_0, out_1):
    nc = tc.nc

    g_hbm = grad_out.rearrange("b g h -> b (g h)").rearrange("(p j) w -> p j w", j=PACK)
    d_hbm = d_x.rearrange("b g h -> b (g h)").rearrange("(p j) w -> p j w", j=PACK)
    w_hbm = w_x.rearrange("g h i -> (g h) i").rearrange("(c p j) i -> p c j i", p=P, j=PACK)
    s_hbm = src_x.rearrange("(p j) i -> p j i", j=PACK)
    o0_hbm = out_0.rearrange("(p j) i -> p j i", j=PACK)
    o1_hbm = out_1.rearrange("g h i -> (g h) i").rearrange("(c m a) i -> m c a i", a=PACK, m=P)

    with ExitStack() as ctx:
        const = ctx.enter_context(tc.tile_pool(name="const", bufs=1))
        inp = ctx.enter_context(tc.tile_pool(name="inp", bufs=1))
        slot = ctx.enter_context(tc.tile_pool(name="slot", bufs=8))
        work3 = ctx.enter_context(tc.tile_pool(name="work3", bufs=3))
        work2 = ctx.enter_context(tc.tile_pool(name="work2", bufs=2))
        ps_acc = ctx.enter_context(tc.psum_pool(name="ps_acc", bufs=1))
        ps_t = ctx.enter_context(tc.psum_pool(name="ps_t", bufs=2))
        ps_o = ctx.enter_context(tc.psum_pool(name="ps_o", bufs=2))

        ident = const.tile([P, P], F32, name="ident")
        make_identity(nc, ident[:])

        g_of, d_of, w_of = [], [], []
        src_raw = inp.tile([P, PACK, IN], BF16, name="src_raw")
        c = 0
        g0_rows, d0_rows = [], []
        for n in LOAD_GROUPS:
            cols = slice(c * CH, (c + n) * CH)
            if c == 0:
                for j in range(PACK):
                    g_r = inp.tile([P, CH], BF16, name="g0r%d" % j)
                    nc.sync.dma_start(out=g_r[:], in_=g_hbm[:, j, cols])
                    d_r = inp.tile([P, CH], F32, name="d0r%d" % j)
                    nc.sync.dma_start(out=d_r[:], in_=d_hbm[:, j, cols])
                    g0_rows.append(g_r)
                    d0_rows.append(d_r)
                g_t, d_t = None, None
                nc.sync.dma_start(out=src_raw[:], in_=s_hbm)
            else:
                if c == 2:
                    g_wide = inp.tile([P, PACK, 2 * CH], BF16, name="g23")
                    nc.sync.dma_start(out=g_wide[:], in_=g_hbm[:, :, 2 * CH : 4 * CH])
                if c == 4:
                    g_wide4 = inp.tile([P, PACK, 4 * CH], BF16, name="g4567")
                    nc.sync.dma_start(out=g_wide4[:], in_=g_hbm[:, :, 4 * CH : 8 * CH])
                if c in (2, 3):
                    g_t = g_wide[:, :, (c - 2) * CH : (c - 1) * CH]
                elif c >= 4:
                    g_t = g_wide4[:, :, (c - 4) * CH : (c - 4 + n) * CH]
                else:
                    g_t = inp.tile([P, PACK, n * CH], BF16, name="g%d" % c)
                    nc.sync.dma_start(out=g_t[:], in_=g_hbm[:, :, cols])
                if n == 1:
                    d_t = slot.tile([P, PACK, CH], F32, name="d%d" % c, tag="slot")
                else:
                    d_t = inp.tile([P, PACK, n * CH], F32, name="d%d" % c)
                nc.sync.dma_start(out=d_t[:], in_=d_hbm[:, :, cols])
            w_t = inp.tile([P, n, PACK, IN], BF16, name="w%d" % c)
            nc.sync.dma_start(out=w_t[:], in_=w_hbm[:, c : c + n])
            for k in range(n):
                g_of.append(None if c == 0 else g_t[:, :, k * CH : (k + 1) * CH])
                d_of.append(None if c == 0 else d_t[:, :, k * CH : (k + 1) * CH])
                w_of.append(w_t[:, k])
            c += n

        acc = [ps_acc.tile([P, IN], F32, name="acc%d" % j) for j in range(PACK)]
        src_codes = const.tile([P, IN], U32, name="src_codes", align_bytes=64)
        src_scales = const.tile([P, IN], U8, name="src_scales", align_bytes=64)

        dz, xts, dzt, dzi, wg = {}, {}, {}, {}, {}
        tok_q, feat_q, w_q = {}, {}, {}

        def mult(i):
            dz[i] = work3.tile([P, PACK, CH], BF16, name="dz", tag="dz")
            if i == 0:
                for j in range(PACK):
                    nc.vector.tensor_tensor(out=dz[i][:, j, :], in0=g0_rows[j][:], in1=d0_rows[j][:], op=mybir.AluOpType.mult)
            else:
                nc.vector.tensor_tensor(out=dz[i][:], in0=g_of[i], in1=d_of[i], op=mybir.AluOpType.mult)

        def interleave_rows(eng_copy, raw):
            grouped = work3.tile([P, IN, PACK], BF16, name="wg", tag="wg", align_bytes=64)
            eng_copy(
                out=grouped[:].rearrange("p (c i) t -> p c t i", i=4),
                in_=raw.rearrange("p t (c i) -> p c t i", i=4),
            )
            return grouped

        def transposes(i):
            xts[i] = []
            for h in range(2):
                xt = ps_t.tile([P, 2, 2, P], F32, name="xt", tag="xt")
                for jj in range(2):
                    words = dz[i][:, 2 * h + jj, :].bitcast(F32)
                    for u in range(2):
                        nc.tensor.transpose(xt[:, jj, u, :], words[:, u : CH // 2 : 2], ident[:])
                xts[i].append(xt)

        def copy_transposed(i):
            dzt[i] = work2.tile([P, B, PACK], BF16, name="dzt", tag="dzt", align_bytes=64)
            tw = dzt[i][:].rearrange("p c t -> p (c t)").bitcast(F32).rearrange("p (j r u) -> p j r u", j=PACK, u=2)
            for h in range(2):
                nc.scalar.copy(out=tw[:, 2 * h : 2 * h + 2], in_=xts[i][h][:].rearrange("p j u r -> p j r u"))

        def interleave_tokens(i):
            dzi[i] = work2.tile([P, CH, PACK], BF16, name="dzi", tag="dzi", align_bytes=64)
            nc.vector.tensor_copy(
                out=dzi[i][:].rearrange("p (a m) j -> p m j a", a=PACK),
                in_=dz[i][:].rearrange("p j (m a) -> p m j a", a=PACK),
            )

        def quantize(grouped, fmt, kind):
            codes = work2.tile([P, CH], U32, name="c" + kind, tag="c" + kind, align_bytes=64)
            scales = work2.tile([P, CH], U8, name="s" + kind, tag="s" + kind, align_bytes=64)
            nc.vector.quantize_mx(out=codes[:].bitcast(fmt), scales=scales[:], in_=grouped[:].rearrange("p w j -> p (w j)"))
            return codes, scales

        def out0_pass(i):
            codes, scales = feat_q[i]
            wc, ws = w_q[i]
            for j in range(PACK):
                m = slice(j * P, (j + 1) * P)
                nc.tensor.matmul_mx(
                    out=acc[j][:],
                    lhsT=codes[:, m].bitcast(E5X4),
                    lhsT_scale=scales[:, m],
                    rhs=wc[:].bitcast(E4X4),
                    rhs_scale=ws[:],
                    start=(i == 0),
                    stop=(i == NCH - 1),
                )

        stages = {}

        def out1_tile(i, a, eng_copy):
            codes, scales = tok_q[i]
            if a == 0:
                stages[i] = slot.tile([P, PACK, IN], F32, name="stage", tag="slot")
            m = slice(a * P, (a + 1) * P)
            o1 = ps_o.tile([P, IN], F32, name="o1", tag="o1")
            nc.tensor.matmul_mx(
                out=o1[:],
                lhsT=codes[:, m].bitcast(E5X4),
                lhsT_scale=scales[:, m],
                rhs=src_codes[:].bitcast(E4X4),
                rhs_scale=src_scales[:],
                start=True,
                stop=True,
            )
            return o1

        def evac1(i, a, o1, eng_copy):
            eng_copy(out=stages[i][:, a, :], in_=o1[:])

        LAST = NCH - 1
        with tc.manual_schedule():
            for i in range(NCH):
                mult(i)
                if i < LAST:
                    wg[i] = interleave_rows(nc.scalar.copy, w_of[i])
                transposes(i)
                copy_transposed(i)
                if i >= 1:
                    feat_q[i - 1] = quantize(dzt[i - 1], E5X4, "f")
                interleave_tokens(i)
                if i == 0:
                    src_g = interleave_rows(nc.vector.tensor_copy, src_raw[:])
                else:
                    w_q[i - 1] = quantize(wg[i - 1], E4X4, "w")
                    out0_pass(i - 1)
                tok_q[i] = quantize(dzi[i], E5X4, "t")
                if i == 0:
                    nc.vector.quantize_mx(
                        out=src_codes[:].bitcast(E4X4), scales=src_scales[:], in_=src_g[:].rearrange("p w j -> p (w j)")
                    )
                if i == LAST:
                    wg[i] = interleave_rows(nc.vector.tensor_copy, w_of[i])
                if i < LAST:
                    for a in range(PACK):
                        evac1(i, a, out1_tile(i, a, None), nc.scalar.copy)
                    nc.sync.dma_start(out=o1_hbm[:, i], in_=stages[i][:])

            for a in range(2):
                evac1(LAST, a, out1_tile(LAST, a, None), nc.scalar.copy)
            nc.sync.dma_start(out=o1_hbm[:, LAST, 0:2], in_=stages[LAST][:, 0:2])
            feat_q[LAST] = quantize(dzt[LAST], E5X4, "f")
            w_q[LAST] = quantize(wg[LAST], E4X4, "w")
            out0_pass(LAST)
            o1_2 = out1_tile(LAST, 2, None)
            o1_3 = out1_tile(LAST, 3, None)
            stage0 = slot.tile([P, PACK, IN], F32, name="stage0", tag="slot")
            nc.vector.tensor_copy(out=stage0[:, 0, :], in_=acc[0][:])
            nc.scalar.copy(out=stage0[:, 2, :], in_=acc[2][:])
            nc.vector.tensor_copy(out=stage0[:, 1, :], in_=acc[1][:])
            nc.scalar.copy(out=stage0[:, 3, :], in_=acc[3][:])
            nc.sync.dma_start(out=o0_hbm[:, 0:2], in_=stage0[:, 0:2])
            nc.sync.dma_start(out=o0_hbm[:, 2:4], in_=stage0[:, 2:4])
            evac1(LAST, 2, o1_2, nc.vector.tensor_copy)
            evac1(LAST, 3, o1_3, nc.scalar.copy)
            nc.sync.dma_start(out=o1_hbm[:, LAST, 2:4], in_=stages[LAST][:, 2:4])
